import numpy as np
import ml_dtypes


def mxq(x, axis, fmt="e4m3"):
    dtype, down = {"e4m3": (ml_dtypes.float8_e4m3fn, 7), "e5m2": (ml_dtypes.float8_e5m2, 14)}[fmt]
    v = np.moveaxis(np.asarray(x, np.float32).astype(ml_dtypes.bfloat16).astype(np.float64), axis, -1)
    blocks = v.reshape(v.shape[:-1] + (-1, 32))
    amax = np.abs(blocks).max(-1, keepdims=True)
    byte = np.maximum(np.where(amax > 0, np.frexp(amax)[1] - 1 + 127, 0) - down, 1)
    scale = np.exp2(byte - 127.0)
    codes = (blocks / scale).astype(np.float32).astype(dtype).astype(np.float64)
    return np.moveaxis((codes * scale).reshape(v.shape), -1, axis)


WIDE = False


def mx_kscale(k):
    if not WIDE:
        return np.ones(k)
    levels = np.array([10, -10, 5, -5, 0])
    a = np.random.permutation(np.resize(levels, k // 512 * 4)).reshape(k // 512, 4)
    idx = np.arange(k)
    return np.exp2(a[idx // 512, idx % 128 // 32])


BF16 = ml_dtypes.bfloat16


def bf(x):
    return np.asarray(x, np.float32).astype(BF16)


def f64(x):
    return np.asarray(x).astype(np.float64)


E2M1 = np.array([0.0, 0.5, 1.0, 1.5, 2.0, 3.0, 4.0, 6.0, -0.0, -0.5, -1.0, -1.5, -2.0, -3.0, -4.0, -6.0])


def pack_weight(w, fmt):
    k, n = w.shape
    w = f64(bf(w)).reshape(k // 32, 32, n)
    amax = np.abs(w).max(1)
    if fmt == "e4m3":
        byte = np.frexp(amax)[1] - 1 + 127 - 7
    else:
        mant, ex = np.frexp(amax / 6.0)
        byte = np.where(mant > 0.5, ex, ex - 1) + 127
    byte = np.clip(np.where(amax > 0, byte, 1), 1, 254)
    scaled = (w * np.exp2(127.0 - byte)[:, None, :]).reshape(k, n).astype(np.float32)
    by_word = np.ascontiguousarray(scaled.reshape(k // 512, 128, 4, n).transpose(0, 1, 3, 2))
    if fmt == "e4m3":
        words = by_word.astype(ml_dtypes.float8_e4m3fn).view(np.uint8)
    else:
        c = by_word.astype(ml_dtypes.float4_e2m1fn).view(np.uint8) & 0xF
        words = c[..., 0::2] | (c[..., 1::2] << 4)
    return np.ascontiguousarray(words), np.ascontiguousarray(byte.astype(np.uint8).reshape(k // 512, 16, n))


def unpack_weight(words, scales, fmt):
    g, p, n, _ = words.shape
    if fmt == "e4m3":
        vals = np.ascontiguousarray(words).view(ml_dtypes.float8_e4m3fn).astype(np.float64)
    else:
        nib = np.empty((g, p, n, 4), np.uint8)
        nib[..., 0::2] = words & 0xF
        nib[..., 1::2] = words >> 4
        vals = E2M1[nib]
    vals = vals * np.repeat(np.exp2(scales.astype(np.float64) - 127.0), 8, axis=1)[..., None]
    return vals.transpose(0, 1, 3, 2).reshape(g * 512, n)


B, N, D, HID, HEADS = 1, 16, 3, 8192, 2048


def silu(v):
    e = np.exp(-np.abs(v))
    return v * np.where(v >= 0, 1.0, e) / (1.0 + e)


def pairwise_dist(c):
    diff = c[:, :, None, :] - c[:, None, :, :]
    sq = np.sum(diff * diff, axis=-1)
    safe = np.where(sq > 0, sq, 1.0)
    return np.where(sq > 0, np.sqrt(safe), 0.0)


def setup_inputs():
    t = np.maximum(mx_kscale(HID), 1.0) ** 2
    coords = bf(np.random.standard_normal((B, N, D)))
    w1 = bf(np.random.uniform(-1.0, 1.0, (1, HID)) * t[None, :])
    b1 = bf(np.random.uniform(-1.0, 1.0, HID) * t)
    w2_words, w2_scales = pack_weight(np.random.standard_normal((HID, HEADS)) / np.sqrt(HID) / t[:, None], "e4m3")
    b2 = bf(np.random.standard_normal(HEADS) * 0.3)
    return {"coords": coords,
            "w1": w1,
            "b1": b1,
            "w2_words": w2_words,
            "w2_scales": w2_scales,
            "b2": b2}


def reference(coords, w1, b1, w2_words, w2_scales, b2):
    d = pairwise_dist(f64(coords))
    h = silu(d[..., None] * f64(w1)[0] + f64(b1))
    b = (mxq(h, 3, "e4m3") @ unpack_weight(w2_words, w2_scales, "e4m3")) + f64(b2)
    return np.transpose(b, (0, 3, 1, 2))

@@ -1,0 +1,229 @@
+import concourse.mybir as mybir
+from concourse.masks import make_identity
+
+F32 = mybir.dt.float32
+BF16 = mybir.dt.bfloat16
+I32 = mybir.dt.int32
+U32 = mybir.dt.uint32
+U8 = mybir.dt.uint8
+FP8X4 = mybir.dt.float8_e4m3fn_x4
+ALU = mybir.AluOpType
+ACT = mybir.ActivationFunctionType
+AX = mybir.AxisListType
+
+P = 128
+NPTS = 16
+HID = 8192
+HEADS = 2048
+GROUPS = HID // 512
+FULL = 272
+SLOTS = 128
+TILES = HEADS // P
+PHASE_TILES = 8
+QUAD = 4
+HG = 2
+TINY = 1e-30
+
+FLOPS = 2 * NPTS * NPTS * HID * HEADS
+
+
+def block_views(full, compact, size):
+    off = 16 - 2 * size
+    comp = compact.rearrange("p (b r q) -> p b r q", r=size, q=16)[:, :, :, off : off + size]
+    by_block = full.rearrange("p (b x) -> p b x", x=34 * size)
+    upper = by_block[:, :, 0 : 16 * size].rearrange("p b (r y) -> p b r y", y=16)[:, :, :, size : 2 * size]
+    lower = by_block[:, :, 16 * size : 32 * size].rearrange("p b (c y) -> p b c y", y=16)[:, :, :, 0:size]
+    return comp, upper, lower
+
+
+def tile_distancerelativebias_w_kernel(tc, coords, w1, b1, w2_words, w2_scales, b2, out):
+    nc = tc.nc
+    with tc.manual_schedule(), tc.tile_pool(name="keep", bufs=1) as keep, tc.tile_pool(
+        name="zpool", bufs=3
+    ) as zpool, tc.tile_pool(name="gpool", bufs=3) as gpool, tc.psum_pool(name="psum", bufs=1) as psum:
+        cb = keep.tile([P, NPTS * 3], BF16, name="cb")
+        nc.sync.dma_start(out=cb[:], in_=coords.rearrange("b n d -> (b n d)").partition_broadcast(P))
+        rows = keep.tile([P, 512], BF16, name="rows")
+        nc.sync.dma_start(out=rows[0:16, :], in_=w1.rearrange("o (g k) -> (o g) k", k=512))
+        nc.sync.dma_start(out=rows[16:32, :], in_=b1.rearrange("(g k) -> g k", k=512))
+        b2rows = keep.tile([16, P], BF16, name="b2rows")
+        nc.sync.dma_start(out=b2rows[:], in_=b2.rearrange("(t p) -> t p", p=P))
+
+        planes = keep.tile([P, 4, HEADS], U8, name="planes", align_bytes=64)
+        one = keep.tile([P, 1], F32, name="one")
+        warm = keep.tile([P, 1], F32, name="warm")
+        nc.vector.memset(one[:], 1.0)
+        nc.scalar.activation(out=warm[:], in_=one[:], func=ACT.Sqrt)
+        for gq in range(4):
+            nc.vector.memset(planes[:, gq, :].bitcast(I32), 0)
+        for gq in range(4):
+            for quad in range(4):
+                nc.sync.dma_start(
+                    out=planes[32 * quad : 32 * quad + 16, gq, :].bitcast(I32),
+                    in_=w2_scales[4 * gq : 4 * gq + 4, 4 * quad : 4 * quad + 4, :].bitcast(I32),
+                )
+
+        words = {}
+        half = 4 * P * PHASE_TILES
+        for ph in range(2):
+            for g in range(GROUPS):
+                wt = keep.tile([P, P * PHASE_TILES], U32, name="w%d_%d" % (ph, g), align_bytes=64)
+                nc.sync.dma_start(
+                    out=wt[:].bitcast(I32),
+                    in_=w2_words[g].rearrange("p n t -> p (n t)")[:, half * ph : half * (ph + 1)].bitcast(I32),
+                )
+                words[(ph, g)] = wt
+
+        nc.gpsimd.memset(rows[32:64, :], 0.0)
+        nc.gpsimd.memset(rows[64:128, :], 0.0)
+        ident = keep.tile([P, P], F32, name="ident")
+        make_identity(nc, ident[:])
+        b2pad = keep.tile([P, P], F32, name="b2pad")
+        nc.gpsimd.memset(b2pad[:], 0.0)
+        nc.vector.tensor_copy(out=b2pad[0:16, :], in_=b2rows[:])
+
+        pro = psum.tile([P, 512], F32, tag="bank0", name="pro")
+        row_words = rows[:].bitcast(F32)
+        for u in range(2):
+            nc.tensor.transpose(pro[:, P * u : P * (u + 1)], row_words[:, u : 256 : 2], ident[:])
+        nc.tensor.transpose(pro[:, 2 * P : 3 * P], b2pad[:], ident[:])
+
+        c3 = cb[:].rearrange("p (n c) -> p n c", c=3)
+        diff = keep.tile([P, NPTS, NPTS, 3], F32, name="diff")
+        nc.vector.tensor_tensor(
+            out=diff[:],
+            in0=c3.unsqueeze(2).to_broadcast([P, NPTS, NPTS, 3]),
+            in1=c3.unsqueeze(1).to_broadcast([P, NPTS, NPTS, 3]),
+            op=ALU.subtract,
+        )
+        nc.vector.tensor_tensor(out=diff[:], in0=diff[:], in1=diff[:], op=ALU.mult)
+        sq_full = keep.tile([P, FULL], F32, name="sq_full")
+        nc.vector.tensor_reduce(
+            out=sq_full[:, 0:256], in_=diff[:].rearrange("p i j c -> p (i j) c"), axis=AX.X, op=ALU.add
+        )
+
+        wb_bf = keep.tile([P, 32, 4], BF16, name="wb_bf")
+        nc.vector.tensor_copy(
+            out=wb_bf[:].rearrange("p r t -> p (r t)").bitcast(F32).rearrange("p (r u) -> p r u", u=2),
+            in_=pro[:, 0 : 2 * P].rearrange("p (u r) -> p r u", u=2)[:, 0:32, :],
+        )
+        wb = keep.tile([P, 128], F32, name="wb")
+        nc.vector.tensor_copy(out=wb[:], in_=wb_bf[:].rearrange("p r t -> p (r t)"))
+        b2col = keep.tile([P, TILES], F32, name="b2col")
+        nc.vector.tensor_copy(out=b2col[:], in_=pro[:, 2 * P : 2 * P + TILES])
+
+        sq = keep.tile([P, SLOTS], F32, name="sq")
+        for size in (8, 4, 2, 1):
+            comp, upper, lower = block_views(sq_full[:], sq[:], size)
+            nc.vector.tensor_copy(out=comp, in_=upper)
+        nc.vector.tensor_copy(
+            out=sq[:].rearrange("p (b q) -> p b q", q=16)[:, :, 15:16],
+            in_=sq_full[:].rearrange("p (b x) -> p b x", x=34)[:, :, 0:1],
+        )
+        safe = keep.tile([P, SLOTS], F32, name="safe")
+        nc.vector.tensor_scalar(out=safe[:], in0=sq[:], scalar1=TINY, scalar2=None, op0=ALU.max)
+        root = keep.tile([P, SLOTS], F32, name="root")
+        nc.scalar.activation(out=root[:], in_=safe[:], func=ACT.Sqrt)
+        dist = keep.tile([P, SLOTS], F32, name="dist")
+        nc.vector.scalar_tensor_tensor(
+            out=dist[:], in0=sq[:], scalar=0.0, in1=root[:], op0=ALU.is_gt, op1=ALU.mult
+        )
+
+        h_codes = keep.tile([P, GROUPS, SLOTS], U32, name="h_codes", align_bytes=64)
+        h_plane = keep.tile([P, GROUPS, SLOTS], U8, name="h_plane", align_bytes=64)
+        z_tiles = {}
+
+        def affine(c):
+            z = zpool.tile([P, HG, 4, SLOTS], F32, name="z")
+            for a in range(HG):
+                for t in range(4):
+                    col = 4 * (HG * c + a) + t
+                    nc.vector.tensor_scalar(
+                        out=z[:, a, t, :],
+                        in0=dist[:],
+                        scalar1=wb[:, col : col + 1],
+                        scalar2=wb[:, 64 + col : 64 + col + 1],
+                        op0=ALU.mult,
+                        op1=ALU.add,
+                    )
+            z_tiles[c] = z
+
+        acc = {}
+
+        def passes(ph, g):
+            for tl in range(PHASE_TILES):
+                if g == 0:
+                    acc[tl] = psum.tile([P, 512], F32, tag="bank%d" % tl, name="acc%d_%d" % (ph, tl))
+                n0 = P * (PHASE_TILES * ph + tl)
+                nc.tensor.matmul_mx(
+                    out=acc[tl][:, 0:SLOTS],
+                    lhsT=words[(ph, g)][:, P * tl : P * (tl + 1)].bitcast(FP8X4),
+                    lhsT_scale=planes[4 * (g % 4) : P, g // 4, n0 : n0 + P],
+                    rhs=h_codes[:, g, :].bitcast(FP8X4),
+                    rhs_scale=h_plane[:, g, :],
+                    start=(g == 0),
+                    stop=(g == GROUPS - 1),
+                )
+
+        out_rows = out.rearrange("b (q t p) i j -> (b q) p t (i j)", t=QUAD, p=P)
+
+        def leave(ph):
+            for hq in range(PHASE_TILES // QUAD):
+                q = (PHASE_TILES // QUAD) * ph + hq
+                compact = keep.tile([P, QUAD * SLOTS], F32, name="compact%d" % q)
+                full = keep.tile([P, QUAD * FULL], F32, name="full%d" % q)
+                for a in range(QUAD):
+                    tl = QUAD * hq + a
+                    bias = b2col[:, QUAD * q + a : QUAD * q + a + 1]
+                    dst = compact[:, SLOTS * a : SLOTS * (a + 1)]
+                    if a % 2 == 0:
+                        nc.scalar.activation(out=dst, in_=acc[tl][:, 0:SLOTS], func=ACT.Identity, bias=bias)
+                    else:
+                        nc.vector.tensor_scalar(
+                            out=dst, in0=acc[tl][:, 0:SLOTS], scalar1=bias, scalar2=None, op0=ALU.add
+                        )
+                comp, upper, lower = block_views(full[:], compact[:], 8)
+                nc.scalar.copy(out=upper, in_=comp)
+                nc.scalar.copy(out=lower, in_=comp.rearrange("p b r c -> p b c r"))
+                for size in (4, 2):
+                    comp, upper, lower = block_views(full[:], compact[:], size)
+                    nc.vector.tensor_copy(out=upper, in_=comp)
+                    nc.vector.tensor_copy(out=lower, in_=comp.rearrange("p b r c -> p b c r"))
+                by_two = full[:].rearrange("p (b x) -> p b x", x=34)
+                slots = compact[:].rearrange("p (b q) -> p b q", q=16)
+                nb = 8 * QUAD
+                nc.vector.tensor_copy(
+                    out=by_two[:, :, 1:31].rearrange("p b (a y) -> p b a y", y=15)[:, :, :, 0:1],
+                    in_=slots[:, :, 14:15].unsqueeze(2).to_broadcast([P, nb, 2, 1]),
+                )
+                nc.vector.tensor_copy(
+                    out=by_two[:, :, 0:34].rearrange("p b (a y) -> p b a y", y=17)[:, :, :, 0:1],
+                    in_=slots[:, :, 15:16].unsqueeze(2).to_broadcast([P, nb, 2, 1]),
+                )
+                nc.sync.dma_start(
+                    out=out_rows[q], in_=full[:].rearrange("p (t x) -> p t x", x=FULL)[:, :, 0:256]
+                )
+
+        chunks = GROUPS // HG
+        affine(0)
+        affine(1)
+        for c in range(chunks):
+            if c + 2 < chunks:
+                affine(c + 2)
+            grouped = gpool.tile([P, HG * 4 * SLOTS], BF16, name="grouped", align_bytes=64)
+            nc.scalar.activation(
+                out=grouped[:].rearrange("p (a u t) -> p a u t", a=HG, t=4),
+                in_=z_tiles[c][:].rearrange("p a t u -> p a u t"),
+                func=ACT.Silu,
+            )
+            nc.vector.quantize_mx(
+                out=h_codes[:, HG * c : HG * (c + 1), :].rearrange("p a u -> p (a u)").bitcast(FP8X4),
+                scales=h_plane[:, HG * c : HG * (c + 1), :].rearrange("p a u -> p (a u)"),
+                in_=grouped[:],
+            )
+            for a in range(HG):
+                passes(0, HG * c + a)
+        leave(0)
+        for g in range(GROUPS):
+            passes(1, g)
+        leave(1)

@@ -22,6 +22,9 @@ TILES = HEADS // P
 PHASE_TILES = 8
 QUAD = 4
 HG = 2
+EARLY = 2
+TAPER = 4
+SW_PLANES = ()
 TINY = 1e-30
 
 FLOPS = 2 * NPTS * NPTS * HID * HEADS
@@ -54,34 +57,52 @@ def tile_distancerelativebias_w_kernel(tc, coords, w1, b1, w2_words, w2_scales, 
         warm = keep.tile([P, 1], F32, name="warm")
         nc.vector.memset(one[:], 1.0)
         nc.scalar.activation(out=warm[:], in_=one[:], func=ACT.Sqrt)
-        for gq in range(4):
+        for gq in SW_PLANES:
             nc.vector.memset(planes[:, gq, :].bitcast(I32), 0)
         for gq in range(4):
-            for quad in range(4):
-                nc.sync.dma_start(
-                    out=planes[32 * quad : 32 * quad + 16, gq, :].bitcast(I32),
-                    in_=w2_scales[4 * gq : 4 * gq + 4, 4 * quad : 4 * quad + 4, :].bitcast(I32),
-                )
+            if gq not in SW_PLANES:
+                nc.vector.memset(planes[:, gq, :].bitcast(I32), 0)
 
-        words = {}
-        half = 4 * P * PHASE_TILES
-        for ph in range(2):
-            for g in range(GROUPS):
-                wt = keep.tile([P, P * PHASE_TILES], U32, name="w%d_%d" % (ph, g), align_bytes=64)
-                nc.sync.dma_start(
-                    out=wt[:].bitcast(I32),
-                    in_=w2_words[g].rearrange("p n t -> p (n t)")[:, half * ph : half * (ph + 1)].bitcast(I32),
-                )
-                words[(ph, g)] = wt
-
-        nc.gpsimd.memset(rows[32:64, :], 0.0)
-        nc.gpsimd.memset(rows[64:128, :], 0.0)
         ident = keep.tile([P, P], F32, name="ident")
         make_identity(nc, ident[:])
+        nc.gpsimd.memset(rows[32:64, :], 0.0)
+        nc.gpsimd.memset(rows[64:128, :], 0.0)
         b2pad = keep.tile([P, P], F32, name="b2pad")
         nc.gpsimd.memset(b2pad[:], 0.0)
-        nc.vector.tensor_copy(out=b2pad[0:16, :], in_=b2rows[:])
 
+        words = {}
+
+        def load_words(g, first, count):
+            wt = keep.tile([P, P * count], U32, name="w%d_%d" % (g, first), align_bytes=64)
+            nc.sync.dma_start(
+                out=wt[:].bitcast(I32),
+                in_=w2_words[g].rearrange("p n t -> p (n t)")[:, 4 * P * first : 4 * P * (first + count)].bitcast(I32),
+            )
+            for tl in range(count):
+                words[(g, first + tl)] = wt[:, P * tl : P * (tl + 1)]
+
+        def load_planes(gq):
+            for quad in range(4):
+                dst = planes[32 * quad : 32 * quad + 16, gq, :]
+                src = w2_scales[4 * gq : 4 * gq + 4, 4 * quad : 4 * quad + 4, :]
+                if gq in SW_PLANES:
+                    nc.gpsimd.dma_start(out=dst.bitcast(F32), in_=src.bitcast(F32))
+                else:
+                    nc.sync.dma_start(out=dst.bitcast(I32), in_=src.bitcast(I32))
+
+        for g in range(EARLY):
+            load_words(g, 0, PHASE_TILES)
+        for gq in range(4):
+            load_planes(gq)
+        for g in range(EARLY, GROUPS):
+            load_words(g, 0, PHASE_TILES)
+        for g in range(GROUPS - TAPER):
+            load_words(g, PHASE_TILES, PHASE_TILES)
+        for first in range(PHASE_TILES, TILES, QUAD):
+            for g in range(GROUPS - TAPER, GROUPS):
+                load_words(g, first, QUAD)
+
+        nc.vector.tensor_copy(out=b2pad[0:16, :], in_=b2rows[:])
         pro = psum.tile([P, 512], F32, tag="bank0", name="pro")
         row_words = rows[:].bitcast(F32)
         for u in range(2):
@@ -150,15 +171,16 @@ def tile_distancerelativebias_w_kernel(tc, coords, w1, b1, w2_words, w2_scales, 
 
         acc = {}
 
-        def passes(ph, g):
-            for tl in range(PHASE_TILES):
+        def passes(g, first, count):
+            for tile_no in range(first, first + count):
                 if g == 0:
-                    acc[tl] = psum.tile([P, 512], F32, tag="bank%d" % tl, name="acc%d_%d" % (ph, tl))
-                n0 = P * (PHASE_TILES * ph + tl)
+                    acc[tile_no] = psum.tile(
+                        [P, 512], F32, tag="bank%d" % (tile_no % PHASE_TILES), name="acc%d" % tile_no
+                    )
                 nc.tensor.matmul_mx(
-                    out=acc[tl][:, 0:SLOTS],
-                    lhsT=words[(ph, g)][:, P * tl : P * (tl + 1)].bitcast(FP8X4),
-                    lhsT_scale=planes[4 * (g % 4) : P, g // 4, n0 : n0 + P],
+                    out=acc[tile_no][:, 0:SLOTS],
+                    lhsT=words[(g, tile_no)].bitcast(FP8X4),
+                    lhsT_scale=planes[4 * (g % 4) : P, g // 4, P * tile_no : P * (tile_no + 1)],
                     rhs=h_codes[:, g, :].bitcast(FP8X4),
                     rhs_scale=h_plane[:, g, :],
                     start=(g == 0),
@@ -167,42 +189,38 @@ def tile_distancerelativebias_w_kernel(tc, coords, w1, b1, w2_words, w2_scales, 
 
         out_rows = out.rearrange("b (q t p) i j -> (b q) p t (i j)", t=QUAD, p=P)
 
-        def leave(ph):
-            for hq in range(PHASE_TILES // QUAD):
-                q = (PHASE_TILES // QUAD) * ph + hq
-                compact = keep.tile([P, QUAD * SLOTS], F32, name="compact%d" % q)
-                full = keep.tile([P, QUAD * FULL], F32, name="full%d" % q)
-                for a in range(QUAD):
-                    tl = QUAD * hq + a
-                    bias = b2col[:, QUAD * q + a : QUAD * q + a + 1]
-                    dst = compact[:, SLOTS * a : SLOTS * (a + 1)]
-                    if a % 2 == 0:
-                        nc.scalar.activation(out=dst, in_=acc[tl][:, 0:SLOTS], func=ACT.Identity, bias=bias)
-                    else:
-                        nc.vector.tensor_scalar(
-                            out=dst, in0=acc[tl][:, 0:SLOTS], scalar1=bias, scalar2=None, op0=ALU.add
-                        )
-                comp, upper, lower = block_views(full[:], compact[:], 8)
-                nc.scalar.copy(out=upper, in_=comp)
-                nc.scalar.copy(out=lower, in_=comp.rearrange("p b r c -> p b c r"))
-                for size in (4, 2):
-                    comp, upper, lower = block_views(full[:], compact[:], size)
-                    nc.vector.tensor_copy(out=upper, in_=comp)
-                    nc.vector.tensor_copy(out=lower, in_=comp.rearrange("p b r c -> p b c r"))
-                by_two = full[:].rearrange("p (b x) -> p b x", x=34)
-                slots = compact[:].rearrange("p (b q) -> p b q", q=16)
-                nb = 8 * QUAD
-                nc.vector.tensor_copy(
-                    out=by_two[:, :, 1:31].rearrange("p b (a y) -> p b a y", y=15)[:, :, :, 0:1],
-                    in_=slots[:, :, 14:15].unsqueeze(2).to_broadcast([P, nb, 2, 1]),
-                )
-                nc.vector.tensor_copy(
-                    out=by_two[:, :, 0:34].rearrange("p b (a y) -> p b a y", y=17)[:, :, :, 0:1],
-                    in_=slots[:, :, 15:16].unsqueeze(2).to_broadcast([P, nb, 2, 1]),
-                )
-                nc.sync.dma_start(
-                    out=out_rows[q], in_=full[:].rearrange("p (t x) -> p t x", x=FULL)[:, :, 0:256]
-                )
+        def leave(q):
+            compact = keep.tile([P, QUAD * SLOTS], F32, name="compact%d" % q)
+            full = keep.tile([P, QUAD * FULL], F32, name="full%d" % q)
+            for a in range(QUAD):
+                tile_no = QUAD * q + a
+                bias = b2col[:, tile_no : tile_no + 1]
+                dst = compact[:, SLOTS * a : SLOTS * (a + 1)]
+                if a % 2 == 0:
+                    nc.scalar.activation(out=dst, in_=acc[tile_no][:, 0:SLOTS], func=ACT.Identity, bias=bias)
+                else:
+                    nc.vector.tensor_scalar(
+                        out=dst, in0=acc[tile_no][:, 0:SLOTS], scalar1=bias, scalar2=None, op0=ALU.add
+                    )
+            comp, upper, lower = block_views(full[:], compact[:], 8)
+            nc.scalar.copy(out=upper, in_=comp)
+            nc.scalar.copy(out=lower, in_=comp.rearrange("p b r c -> p b c r"))
+            for size in (4, 2):
+                comp, upper, lower = block_views(full[:], compact[:], size)
+                nc.vector.tensor_copy(out=upper, in_=comp)
+                nc.vector.tensor_copy(out=lower, in_=comp.rearrange("p b r c -> p b c r"))
+            by_two = full[:].rearrange("p (b x) -> p b x", x=34)
+            slots = compact[:].rearrange("p (b q) -> p b q", q=16)
+            nb = 8 * QUAD
+            nc.vector.tensor_copy(
+                out=by_two[:, :, 1:31].rearrange("p b (a y) -> p b a y", y=15)[:, :, :, 0:1],
+                in_=slots[:, :, 14:15].unsqueeze(2).to_broadcast([P, nb, 2, 1]),
+            )
+            nc.vector.tensor_copy(
+                out=by_two[:, :, 0:34].rearrange("p b (a y) -> p b a y", y=17)[:, :, :, 0:1],
+                in_=slots[:, :, 15:16].unsqueeze(2).to_broadcast([P, nb, 2, 1]),
+            )
+            nc.sync.dma_start(out=out_rows[q], in_=full[:].rearrange("p (t x) -> p t x", x=FULL)[:, :, 0:256])
 
         chunks = GROUPS // HG
         affine(0)
@@ -222,8 +240,12 @@ def tile_distancerelativebias_w_kernel(tc, coords, w1, b1, w2_words, w2_scales, 
                 in_=grouped[:],
             )
             for a in range(HG):
-                passes(0, HG * c + a)
+                passes(HG * c + a, 0, PHASE_TILES)
         leave(0)
-        for g in range(GROUPS):
-            passes(1, g)
         leave(1)
+        for g in range(GROUPS - TAPER):
+            passes(g, PHASE_TILES, PHASE_TILES)
+        for q in (2, 3):
+            for g in range(GROUPS - TAPER, GROUPS):
+                passes(g, QUAD * q, QUAD)
+            leave(q)

@@ -22,9 +22,9 @@ TILES = HEADS // P
 PHASE_TILES = 8
 QUAD = 4
 HG = 2
-EARLY = 2
+EARLY = 0
 TAPER = 4
-SW_PLANES = ()
+SW_PLANES = (0, 1, 2, 3)
 TINY = 1e-30
 
 FLOPS = 2 * NPTS * NPTS * HID * HEADS
@@ -65,10 +65,10 @@ def tile_distancerelativebias_w_kernel(tc, coords, w1, b1, w2_words, w2_scales, 
 
         ident = keep.tile([P, P], F32, name="ident")
         make_identity(nc, ident[:])
-        nc.gpsimd.memset(rows[32:64, :], 0.0)
-        nc.gpsimd.memset(rows[64:128, :], 0.0)
+        nc.vector.memset(rows[32:64, :], 0.0)
+        nc.vector.memset(rows[64:128, :], 0.0)
         b2pad = keep.tile([P, P], F32, name="b2pad")
-        nc.gpsimd.memset(b2pad[:], 0.0)
+        nc.vector.memset(b2pad[:], 0.0)
 
         words = {}
 

@@ -19,11 +19,11 @@ GROUPS = HID // 512
 FULL = 272
 SLOTS = 128
 TILES = HEADS // P
-PHASE_TILES = 8
+BANK_TILES = 2
 QUAD = 4
 HG = 2
 EARLY = 0
-TAPER = 4
+TAPER = 3
 SW_PLANES = (0, 1, 2, 3)
 TINY = 1e-30
 
@@ -91,14 +91,12 @@ def tile_distancerelativebias_w_kernel(tc, coords, w1, b1, w2_words, w2_scales, 
                     nc.sync.dma_start(out=dst.bitcast(I32), in_=src.bitcast(I32))
 
         for g in range(EARLY):
-            load_words(g, 0, PHASE_TILES)
+            load_words(g, 0, TILES)
         for gq in range(4):
             load_planes(gq)
-        for g in range(EARLY, GROUPS):
-            load_words(g, 0, PHASE_TILES)
-        for g in range(GROUPS - TAPER):
-            load_words(g, PHASE_TILES, PHASE_TILES)
-        for first in range(PHASE_TILES, TILES, QUAD):
+        for g in range(EARLY, GROUPS - TAPER):
+            load_words(g, 0, TILES)
+        for first in range(0, TILES, QUAD):
             for g in range(GROUPS - TAPER, GROUPS):
                 load_words(g, first, QUAD)
 
@@ -173,18 +171,19 @@ def tile_distancerelativebias_w_kernel(tc, coords, w1, b1, w2_words, w2_scales, 
 
         def passes(g, first, count):
             for tile_no in range(first, first + count):
-                if g == 0:
-                    acc[tile_no] = psum.tile(
-                        [P, 512], F32, tag="bank%d" % (tile_no % PHASE_TILES), name="acc%d" % tile_no
-                    )
+                place = tile_no % BANK_TILES
+                if g == 0 and place == 0:
+                    bank = psum.tile([P, 512], F32, tag="bank%d" % (tile_no // BANK_TILES), name="acc%d" % tile_no)
+                    for k in range(BANK_TILES):
+                        acc[tile_no + k] = bank[:, SLOTS * k : SLOTS * (k + 1)]
                 nc.tensor.matmul_mx(
-                    out=acc[tile_no][:, 0:SLOTS],
+                    out=acc[tile_no],
                     lhsT=words[(g, tile_no)].bitcast(FP8X4),
                     lhsT_scale=planes[4 * (g % 4) : P, g // 4, P * tile_no : P * (tile_no + 1)],
                     rhs=h_codes[:, g, :].bitcast(FP8X4),
                     rhs_scale=h_plane[:, g, :],
-                    start=(g == 0),
-                    stop=(g == GROUPS - 1),
+                    start=(g == 0 and place == 0),
+                    stop=(g == GROUPS - 1 and place == BANK_TILES - 1),
                 )
 
         out_rows = out.rearrange("b (q t p) i j -> (b q) p t (i j)", t=QUAD, p=P)
@@ -196,12 +195,10 @@ def tile_distancerelativebias_w_kernel(tc, coords, w1, b1, w2_words, w2_scales, 
                 tile_no = QUAD * q + a
                 bias = b2col[:, tile_no : tile_no + 1]
                 dst = compact[:, SLOTS * a : SLOTS * (a + 1)]
-                if a % 2 == 0:
-                    nc.scalar.activation(out=dst, in_=acc[tile_no][:, 0:SLOTS], func=ACT.Identity, bias=bias)
+                if a < BANK_TILES:
+                    nc.scalar.activation(out=dst, in_=acc[tile_no], func=ACT.Identity, bias=bias)
                 else:
-                    nc.vector.tensor_scalar(
-                        out=dst, in0=acc[tile_no][:, 0:SLOTS], scalar1=bias, scalar2=None, op0=ALU.add
-                    )
+                    nc.vector.tensor_scalar(out=dst, in0=acc[tile_no], scalar1=bias, scalar2=None, op0=ALU.add)
             comp, upper, lower = block_views(full[:], compact[:], 8)
             nc.scalar.copy(out=upper, in_=comp)
             nc.scalar.copy(out=lower, in_=comp.rearrange("p b r c -> p b c r"))
@@ -240,12 +237,9 @@ def tile_distancerelativebias_w_kernel(tc, coords, w1, b1, w2_words, w2_scales, 
                 in_=grouped[:],
             )
             for a in range(HG):
-                passes(HG * c + a, 0, PHASE_TILES)
-        leave(0)
-        leave(1)
-        for g in range(GROUPS - TAPER):
-            passes(g, PHASE_TILES, PHASE_TILES)
-        for q in (2, 3):
+                if HG * c + a < GROUPS - TAPER:
+                    passes(HG * c + a, 0, TILES)
+        for q in range(TILES // QUAD):
             for g in range(GROUPS - TAPER, GROUPS):
                 passes(g, QUAD * q, QUAD)
             leave(q)

@@ -20,10 +20,10 @@ FULL = 272
 SLOTS = 128
 TILES = HEADS // P
 BANK_TILES = 2
-QUAD = 4
+UNITS = ((0, 4), (4, 4), (8, 4), (12, 2), (14, 2))
 HG = 2
 EARLY = 0
-TAPER = 3
+TAPER = 4
 SW_PLANES = (0, 1, 2, 3)
 TINY = 1e-30
 
@@ -45,12 +45,12 @@ def tile_distancerelativebias_w_kernel(tc, coords, w1, b1, w2_words, w2_scales, 
         name="zpool", bufs=3
     ) as zpool, tc.tile_pool(name="gpool", bufs=3) as gpool, tc.psum_pool(name="psum", bufs=1) as psum:
         cb = keep.tile([P, NPTS * 3], BF16, name="cb")
-        nc.sync.dma_start(out=cb[:], in_=coords.rearrange("b n d -> (b n d)").partition_broadcast(P))
+        nc.scalar.dma_start(out=cb[:], in_=coords.rearrange("b n d -> (b n d)").partition_broadcast(P))
         rows = keep.tile([P, 512], BF16, name="rows")
-        nc.sync.dma_start(out=rows[0:16, :], in_=w1.rearrange("o (g k) -> (o g) k", k=512))
-        nc.sync.dma_start(out=rows[16:32, :], in_=b1.rearrange("(g k) -> g k", k=512))
+        nc.scalar.dma_start(out=rows[0:16, :], in_=w1.rearrange("o (g k) -> (o g) k", k=512))
+        nc.scalar.dma_start(out=rows[16:32, :], in_=b1.rearrange("(g k) -> g k", k=512))
         b2rows = keep.tile([16, P], BF16, name="b2rows")
-        nc.sync.dma_start(out=b2rows[:], in_=b2.rearrange("(t p) -> t p", p=P))
+        nc.scalar.dma_start(out=b2rows[:], in_=b2.rearrange("(t p) -> t p", p=P))
 
         planes = keep.tile([P, 4, HEADS], U8, name="planes", align_bytes=64)
         one = keep.tile([P, 1], F32, name="one")
@@ -72,14 +72,15 @@ def tile_distancerelativebias_w_kernel(tc, coords, w1, b1, w2_words, w2_scales, 
 
         words = {}
 
-        def load_words(g, first, count):
-            wt = keep.tile([P, P * count], U32, name="w%d_%d" % (g, first), align_bytes=64)
+        def load_words(g0, g1, first, count):
+            wt = keep.tile([P, g1 - g0, P * count], U32, name="w%d_%d" % (g0, first), align_bytes=64)
+            src = w2_words[g0:g1].rearrange("g p n t -> p g (n t)")
             nc.sync.dma_start(
-                out=wt[:].bitcast(I32),
-                in_=w2_words[g].rearrange("p n t -> p (n t)")[:, 4 * P * first : 4 * P * (first + count)].bitcast(I32),
+                out=wt[:].bitcast(I32), in_=src[:, :, 4 * P * first : 4 * P * (first + count)].bitcast(I32)
             )
-            for tl in range(count):
-                words[(g, first + tl)] = wt[:, P * tl : P * (tl + 1)]
+            for g in range(g0, g1):
+                for tl in range(count):
+                    words[(g, first + tl)] = wt[:, g - g0, P * tl : P * (tl + 1)]
 
         def load_planes(gq):
             for quad in range(4):
@@ -91,14 +92,14 @@ def tile_distancerelativebias_w_kernel(tc, coords, w1, b1, w2_words, w2_scales, 
                     nc.sync.dma_start(out=dst.bitcast(I32), in_=src.bitcast(I32))
 
         for g in range(EARLY):
-            load_words(g, 0, TILES)
+            load_words(g, g + 1, 0, TILES)
         for gq in range(4):
             load_planes(gq)
         for g in range(EARLY, GROUPS - TAPER):
-            load_words(g, 0, TILES)
-        for first in range(0, TILES, QUAD):
-            for g in range(GROUPS - TAPER, GROUPS):
-                load_words(g, first, QUAD)
+            load_words(g, g + 1, 0, TILES)
+        for first, count in UNITS:
+            load_words(GROUPS - TAPER, GROUPS - 1, first, count)
+            load_words(GROUPS - 1, GROUPS, first, count)
 
         nc.vector.tensor_copy(out=b2pad[0:16, :], in_=b2rows[:])
         pro = psum.tile([P, 512], F32, tag="bank0", name="pro")
@@ -186,16 +187,16 @@ def tile_distancerelativebias_w_kernel(tc, coords, w1, b1, w2_words, w2_scales, 
                     stop=(g == GROUPS - 1 and place == BANK_TILES - 1),
                 )
 
-        out_rows = out.rearrange("b (q t p) i j -> (b q) p t (i j)", t=QUAD, p=P)
+        out_rows = out.rearrange("b (t p) i j -> p (b t) (i j)", p=P)
 
-        def leave(q):
-            compact = keep.tile([P, QUAD * SLOTS], F32, name="compact%d" % q)
-            full = keep.tile([P, QUAD * FULL], F32, name="full%d" % q)
-            for a in range(QUAD):
-                tile_no = QUAD * q + a
+        def leave(first, count):
+            compact = keep.tile([P, count * SLOTS], F32, name="compact%d" % first)
+            full = keep.tile([P, count * FULL], F32, name="full%d" % first)
+            for a in range(count):
+                tile_no = first + a
                 bias = b2col[:, tile_no : tile_no + 1]
                 dst = compact[:, SLOTS * a : SLOTS * (a + 1)]
-                if a < BANK_TILES:
+                if (tile_no // BANK_TILES) % 2 == 0:
                     nc.scalar.activation(out=dst, in_=acc[tile_no], func=ACT.Identity, bias=bias)
                 else:
                     nc.vector.tensor_scalar(out=dst, in0=acc[tile_no], scalar1=bias, scalar2=None, op0=ALU.add)
@@ -208,7 +209,7 @@ def tile_distancerelativebias_w_kernel(tc, coords, w1, b1, w2_words, w2_scales, 
                 nc.vector.tensor_copy(out=lower, in_=comp.rearrange("p b r c -> p b c r"))
             by_two = full[:].rearrange("p (b x) -> p b x", x=34)
             slots = compact[:].rearrange("p (b q) -> p b q", q=16)
-            nb = 8 * QUAD
+            nb = 8 * count
             nc.vector.tensor_copy(
                 out=by_two[:, :, 1:31].rearrange("p b (a y) -> p b a y", y=15)[:, :, :, 0:1],
                 in_=slots[:, :, 14:15].unsqueeze(2).to_broadcast([P, nb, 2, 1]),
@@ -217,7 +218,10 @@ def tile_distancerelativebias_w_kernel(tc, coords, w1, b1, w2_words, w2_scales, 
                 out=by_two[:, :, 0:34].rearrange("p b (a y) -> p b a y", y=17)[:, :, :, 0:1],
                 in_=slots[:, :, 15:16].unsqueeze(2).to_broadcast([P, nb, 2, 1]),
             )
-            nc.sync.dma_start(out=out_rows[q], in_=full[:].rearrange("p (t x) -> p t x", x=FULL)[:, :, 0:256])
+            nc.sync.dma_start(
+                out=out_rows[:, first : first + count, :],
+                in_=full[:].rearrange("p (t x) -> p t x", x=FULL)[:, :, 0:256],
+            )
 
         chunks = GROUPS // HG
         affine(0)
@@ -239,7 +243,7 @@ def tile_distancerelativebias_w_kernel(tc, coords, w1, b1, w2_words, w2_scales, 
             for a in range(HG):
                 if HG * c + a < GROUPS - TAPER:
                     passes(HG * c + a, 0, TILES)
-        for q in range(TILES // QUAD):
+        for first, count in UNITS:
             for g in range(GROUPS - TAPER, GROUPS):
-                passes(g, QUAD * q, QUAD)
-            leave(q)
+                passes(g, first, count)
+            leave(first, count)

@@ -23,7 +23,8 @@ BANK_TILES = 2
 UNITS = ((0, 4), (4, 4), (8, 4), (12, 2), (14, 2))
 HG = 2
 EARLY = 0
-TAPER = 4
+CUT = {9: 4, 10: 8, 11: 8, 12: 12, 13: 12, 14: 14, 15: 14}
+WHOLE = GROUPS - len(CUT)
 SW_PLANES = (0, 1, 2, 3)
 TINY = 1e-30
 
@@ -95,11 +96,12 @@ def tile_distancerelativebias_w_kernel(tc, coords, w1, b1, w2_words, w2_scales, 
             load_words(g, g + 1, 0, TILES)
         for gq in range(4):
             load_planes(gq)
-        for g in range(EARLY, GROUPS - TAPER):
+        for g in range(EARLY, WHOLE):
             load_words(g, g + 1, 0, TILES)
-        for first, count in UNITS:
-            load_words(GROUPS - TAPER, GROUPS - 1, first, count)
-            load_words(GROUPS - 1, GROUPS, first, count)
+        for g in range(WHOLE, GROUPS):
+            load_words(g, g + 1, 0, CUT[g])
+        for g in range(WHOLE, GROUPS):
+            load_words(g, g + 1, CUT[g], TILES - CUT[g])
 
         nc.vector.tensor_copy(out=b2pad[0:16, :], in_=b2rows[:])
         pro = psum.tile([P, 512], F32, tag="bank0", name="pro")
@@ -169,6 +171,10 @@ def tile_distancerelativebias_w_kernel(tc, coords, w1, b1, w2_words, w2_scales, 
             z_tiles[c] = z
 
         acc = {}
+        last_pass = {}
+        for tile_no in range(TILES):
+            late = [g for g in range(WHOLE, GROUPS) if tile_no >= CUT[g]]
+            last_pass[tile_no] = late[-1] if late else GROUPS - 1
 
         def passes(g, first, count):
             for tile_no in range(first, first + count):
@@ -184,7 +190,7 @@ def tile_distancerelativebias_w_kernel(tc, coords, w1, b1, w2_words, w2_scales, 
                     rhs=h_codes[:, g, :].bitcast(FP8X4),
                     rhs_scale=h_plane[:, g, :],
                     start=(g == 0 and place == 0),
-                    stop=(g == GROUPS - 1 and place == BANK_TILES - 1),
+                    stop=(g == last_pass[tile_no] and place == BANK_TILES - 1),
                 )
 
         out_rows = out.rearrange("b (t p) i j -> p (b t) (i j)", p=P)
@@ -241,9 +247,15 @@ def tile_distancerelativebias_w_kernel(tc, coords, w1, b1, w2_words, w2_scales, 
                 in_=grouped[:],
             )
             for a in range(HG):
-                if HG * c + a < GROUPS - TAPER:
+                if HG * c + a < WHOLE:
                     passes(HG * c + a, 0, TILES)
-        for first, count in UNITS:
-            for g in range(GROUPS - TAPER, GROUPS):
-                passes(g, first, count)
-            leave(first, count)
+        pieces = [(g, 0, CUT[g]) for g in range(WHOLE, GROUPS)] + [(g, CUT[g], TILES) for g in range(WHOLE, GROUPS)]
+        for g, lo, hi in pieces:
+            at = lo
+            for first, count in UNITS:
+                if lo <= first < hi and last_pass[first] == g:
+                    passes(g, at, first + count - at)
+                    at = first + count
+                    leave(first, count)
+            if at < hi:
+                passes(g, at, hi - at)

@@ -53,7 +53,7 @@ def tile_distancerelativebias_w_kernel(tc, coords, w1, b1, w2_words, w2_scales, 
         b2rows = keep.tile([16, P], BF16, name="b2rows")
         nc.scalar.dma_start(out=b2rows[:], in_=b2.rearrange("(t p) -> t p", p=P))
 
-        planes = keep.tile([P, 4, HEADS], U8, name="planes", align_bytes=64)
+        planes = keep.tile([P, 4, HEADS], U8, name="planes", align_bytes=256)
         one = keep.tile([P, 1], F32, name="one")
         warm = keep.tile([P, 1], F32, name="warm")
         nc.vector.memset(one[:], 1.0)
@@ -74,7 +74,7 @@ def tile_distancerelativebias_w_kernel(tc, coords, w1, b1, w2_words, w2_scales, 
         words = {}
 
         def load_words(g0, g1, first, count):
-            wt = keep.tile([P, g1 - g0, P * count], U32, name="w%d_%d" % (g0, first), align_bytes=64)
+            wt = keep.tile([P, g1 - g0, P * count], U32, name="w%d_%d" % (g0, first), align_bytes=256)
             src = w2_words[g0:g1].rearrange("g p n t -> p g (n t)")
             nc.sync.dma_start(
                 out=wt[:].bitcast(I32), in_=src[:, :, 4 * P * first : 4 * P * (first + count)].bitcast(I32)
@@ -197,7 +197,7 @@ def tile_distancerelativebias_w_kernel(tc, coords, w1, b1, w2_words, w2_scales, 
 
         def leave(first, count):
             compact = keep.tile([P, count * SLOTS], F32, name="compact%d" % first)
-            full = keep.tile([P, count * FULL], F32, name="full%d" % first)
+            full = keep.tile([P, count * FULL], F32, name="full%d" % first, align_bytes=256)
             for a in range(count):
                 tile_no = first + a
                 bias = b2col[:, tile_no : tile_no + 1]

@@ -16,7 +16,7 @@ NPTS = 16
 HID = 8192
 HEADS = 2048
 GROUPS = HID // 512
-FULL = 272
+FULL = 1088
 SLOTS = 128
 TILES = HEADS // P
 BANK_TILES = 2
@@ -33,18 +33,17 @@ FLOPS = 2 * NPTS * NPTS * HID * HEADS
 
 def block_views(full, compact, size):
     off = 16 - 2 * size
-    comp = compact.rearrange("p (b r q) -> p b r q", r=size, q=16)[:, :, :, off : off + size]
-    by_block = full.rearrange("p (b x) -> p b x", x=34 * size)
-    upper = by_block[:, :, 0 : 16 * size].rearrange("p b (r y) -> p b r y", y=16)[:, :, :, size : 2 * size]
-    lower = by_block[:, :, 16 * size : 32 * size].rearrange("p b (c y) -> p b c y", y=16)[:, :, :, 0:size]
+    nb = 8 // size
+    comp = compact.rearrange("p (m b r q) -> p m b r q", b=nb, r=size, q=16)[:, :, :, :, off : off + size]
+    by_block = full.rearrange("p (m s x) -> p m s x", s=4 * nb, x=34 * size)[:, :, 0:nb, :]
+    upper = by_block[:, :, :, 0 : 16 * size].rearrange("p m b (r y) -> p m b r y", y=16)[:, :, :, :, size : 2 * size]
+    lower = by_block[:, :, :, 16 * size : 32 * size].rearrange("p m b (c y) -> p m b c y", y=16)[:, :, :, :, 0:size]
     return comp, upper, lower
 
 
 def tile_distancerelativebias_w_kernel(tc, coords, w1, b1, w2_words, w2_scales, b2, out):
     nc = tc.nc
-    with tc.manual_schedule(), tc.tile_pool(name="keep", bufs=1) as keep, tc.tile_pool(
-        name="zpool", bufs=3
-    ) as zpool, tc.tile_pool(name="gpool", bufs=3) as gpool, tc.psum_pool(name="psum", bufs=1) as psum:
+    with tc.manual_schedule(), tc.tile_pool(name="keep", bufs=1) as keep, tc.psum_pool(name="psum", bufs=1) as psum:
         cb = keep.tile([P, NPTS * 3], BF16, name="cb")
         nc.scalar.dma_start(out=cb[:], in_=coords.rearrange("b n d -> (b n d)").partition_broadcast(P))
         rows = keep.tile([P, 512], BF16, name="rows")
@@ -110,38 +109,39 @@ def tile_distancerelativebias_w_kernel(tc, coords, w1, b1, w2_words, w2_scales, 
             nc.tensor.transpose(pro[:, P * u : P * (u + 1)], row_words[:, u : 256 : 2], ident[:])
         nc.tensor.transpose(pro[:, 2 * P : 3 * P], b2pad[:], ident[:])
 
-        c3 = cb[:].rearrange("p (n c) -> p n c", c=3)
-        diff = keep.tile([P, NPTS, NPTS, 3], F32, name="diff")
-        nc.vector.tensor_tensor(
-            out=diff[:],
-            in0=c3.unsqueeze(2).to_broadcast([P, NPTS, NPTS, 3]),
-            in1=c3.unsqueeze(1).to_broadcast([P, NPTS, NPTS, 3]),
-            op=ALU.subtract,
-        )
-        nc.vector.tensor_tensor(out=diff[:], in0=diff[:], in1=diff[:], op=ALU.mult)
-        sq_full = keep.tile([P, FULL], F32, name="sq_full")
-        nc.vector.tensor_reduce(
-            out=sq_full[:, 0:256], in_=diff[:].rearrange("p i j c -> p (i j) c"), axis=AX.X, op=ALU.add
-        )
+        with tc.tile_pool(name="dpool", bufs=1) as dpool:
+            c3 = cb[:].rearrange("p (n c) -> p n c", c=3)
+            diff = dpool.tile([P, NPTS, NPTS, 3], F32, name="diff")
+            nc.vector.tensor_tensor(
+                out=diff[:],
+                in0=c3.unsqueeze(2).to_broadcast([P, NPTS, NPTS, 3]),
+                in1=c3.unsqueeze(1).to_broadcast([P, NPTS, NPTS, 3]),
+                op=ALU.subtract,
+            )
+            nc.vector.tensor_tensor(out=diff[:], in0=diff[:], in1=diff[:], op=ALU.mult)
+            sq_full = dpool.tile([P, FULL], F32, name="sq_full")
+            nc.vector.tensor_reduce(
+                out=sq_full[:, 0:256], in_=diff[:].rearrange("p i j c -> p (i j) c"), axis=AX.X, op=ALU.add
+            )
 
-        wb_bf = keep.tile([P, 32, 4], BF16, name="wb_bf")
-        nc.vector.tensor_copy(
-            out=wb_bf[:].rearrange("p r t -> p (r t)").bitcast(F32).rearrange("p (r u) -> p r u", u=2),
-            in_=pro[:, 0 : 2 * P].rearrange("p (u r) -> p r u", u=2)[:, 0:32, :],
-        )
-        wb = keep.tile([P, 128], F32, name="wb")
-        nc.vector.tensor_copy(out=wb[:], in_=wb_bf[:].rearrange("p r t -> p (r t)"))
-        b2col = keep.tile([P, TILES], F32, name="b2col")
-        nc.vector.tensor_copy(out=b2col[:], in_=pro[:, 2 * P : 2 * P + TILES])
+            wb_bf = keep.tile([P, 32, 4], BF16, name="wb_bf")
+            nc.vector.tensor_copy(
+                out=wb_bf[:].rearrange("p r t -> p (r t)").bitcast(F32).rearrange("p (r u) -> p r u", u=2),
+                in_=pro[:, 0 : 2 * P].rearrange("p (u r) -> p r u", u=2)[:, 0:32, :],
+            )
+            wb = keep.tile([P, 128], F32, name="wb")
+            nc.vector.tensor_copy(out=wb[:], in_=wb_bf[:].rearrange("p r t -> p (r t)"))
+            b2col = keep.tile([P, TILES], F32, name="b2col")
+            nc.vector.tensor_copy(out=b2col[:], in_=pro[:, 2 * P : 2 * P + TILES])
 
-        sq = keep.tile([P, SLOTS], F32, name="sq")
-        for size in (8, 4, 2, 1):
-            comp, upper, lower = block_views(sq_full[:], sq[:], size)
-            nc.vector.tensor_copy(out=comp, in_=upper)
-        nc.vector.tensor_copy(
-            out=sq[:].rearrange("p (b q) -> p b q", q=16)[:, :, 15:16],
-            in_=sq_full[:].rearrange("p (b x) -> p b x", x=34)[:, :, 0:1],
-        )
+            sq = keep.tile([P, SLOTS], F32, name="sq")
+            for size in (8, 4, 2, 1):
+                comp, upper, lower = block_views(sq_full[:], sq[:], size)
+                nc.vector.tensor_copy(out=comp, in_=upper)
+            nc.vector.tensor_copy(
+                out=sq[:].rearrange("p (b q) -> p b q", q=16)[:, :, 15:16],
+                in_=sq_full[:].rearrange("p (b x) -> p b x", x=34)[:, 0:8, 0:1],
+            )
         safe = keep.tile([P, SLOTS], F32, name="safe")
         nc.vector.tensor_scalar(out=safe[:], in0=sq[:], scalar1=TINY, scalar2=None, op0=ALU.max)
         root = keep.tile([P, SLOTS], F32, name="root")
@@ -155,7 +155,7 @@ def tile_distancerelativebias_w_kernel(tc, coords, w1, b1, w2_words, w2_scales, 
         h_plane = keep.tile([P, GROUPS, SLOTS], U8, name="h_plane", align_bytes=64)
         z_tiles = {}
 
-        def affine(c):
+        def affine(zpool, c):
             z = zpool.tile([P, HG, 4, SLOTS], F32, name="z")
             for a in range(HG):
                 for t in range(4):
@@ -195,9 +195,9 @@ def tile_distancerelativebias_w_kernel(tc, coords, w1, b1, w2_words, w2_scales, 
 
         out_rows = out.rearrange("b (t p) i j -> p (b t) (i j)", p=P)
 
-        def leave(first, count):
+        def leave(fpool, first, count):
             compact = keep.tile([P, count * SLOTS], F32, name="compact%d" % first)
-            full = keep.tile([P, count * FULL], F32, name="full%d" % first, align_bytes=256)
+            full = fpool.tile([P, count * FULL], F32, name="full%d" % first, align_bytes=256)
             for a in range(count):
                 tile_no = first + a
                 bias = b2col[:, tile_no : tile_no + 1]
@@ -208,21 +208,20 @@ def tile_distancerelativebias_w_kernel(tc, coords, w1, b1, w2_words, w2_scales, 
                     nc.vector.tensor_scalar(out=dst, in0=acc[tile_no], scalar1=bias, scalar2=None, op0=ALU.add)
             comp, upper, lower = block_views(full[:], compact[:], 8)
             nc.scalar.copy(out=upper, in_=comp)
-            nc.scalar.copy(out=lower, in_=comp.rearrange("p b r c -> p b c r"))
+            nc.scalar.copy(out=lower, in_=comp.rearrange("p m b r c -> p m b c r"))
             for size in (4, 2):
                 comp, upper, lower = block_views(full[:], compact[:], size)
                 nc.vector.tensor_copy(out=upper, in_=comp)
-                nc.vector.tensor_copy(out=lower, in_=comp.rearrange("p b r c -> p b c r"))
-            by_two = full[:].rearrange("p (b x) -> p b x", x=34)
-            slots = compact[:].rearrange("p (b q) -> p b q", q=16)
-            nb = 8 * count
+                nc.vector.tensor_copy(out=lower, in_=comp.rearrange("p m b r c -> p m b c r"))
+            by_two = full[:].rearrange("p (m s x) -> p m s x", s=32, x=34)[:, :, 0:8, :]
+            slots = compact[:].rearrange("p (m b q) -> p m b q", b=8, q=16)
             nc.vector.tensor_copy(
-                out=by_two[:, :, 1:31].rearrange("p b (a y) -> p b a y", y=15)[:, :, :, 0:1],
-                in_=slots[:, :, 14:15].unsqueeze(2).to_broadcast([P, nb, 2, 1]),
+                out=by_two[:, :, :, 1:31].rearrange("p m b (a y) -> p m b a y", y=15)[:, :, :, :, 0:1],
+                in_=slots[:, :, :, 14:15].unsqueeze(3).to_broadcast([P, count, 8, 2, 1]),
             )
             nc.vector.tensor_copy(
-                out=by_two[:, :, 0:34].rearrange("p b (a y) -> p b a y", y=17)[:, :, :, 0:1],
-                in_=slots[:, :, 15:16].unsqueeze(2).to_broadcast([P, nb, 2, 1]),
+                out=by_two[:, :, :, 0:34].rearrange("p m b (a y) -> p m b a y", y=17)[:, :, :, :, 0:1],
+                in_=slots[:, :, :, 15:16].unsqueeze(3).to_broadcast([P, count, 8, 2, 1]),
             )
             nc.sync.dma_start(
                 out=out_rows[:, first : first + count, :],
@@ -230,32 +229,34 @@ def tile_distancerelativebias_w_kernel(tc, coords, w1, b1, w2_words, w2_scales, 
             )
 
         chunks = GROUPS // HG
-        affine(0)
-        affine(1)
-        for c in range(chunks):
-            if c + 2 < chunks:
-                affine(c + 2)
-            grouped = gpool.tile([P, HG * 4 * SLOTS], BF16, name="grouped", align_bytes=64)
-            nc.scalar.activation(
-                out=grouped[:].rearrange("p (a u t) -> p a u t", a=HG, t=4),
-                in_=z_tiles[c][:].rearrange("p a t u -> p a u t"),
-                func=ACT.Silu,
-            )
-            nc.vector.quantize_mx(
-                out=h_codes[:, HG * c : HG * (c + 1), :].rearrange("p a u -> p (a u)").bitcast(FP8X4),
-                scales=h_plane[:, HG * c : HG * (c + 1), :].rearrange("p a u -> p (a u)"),
-                in_=grouped[:],
-            )
-            for a in range(HG):
-                if HG * c + a < WHOLE:
-                    passes(HG * c + a, 0, TILES)
+        with tc.tile_pool(name="zpool", bufs=3) as zpool, tc.tile_pool(name="gpool", bufs=3) as gpool:
+            affine(zpool, 0)
+            affine(zpool, 1)
+            for c in range(chunks):
+                if c + 2 < chunks:
+                    affine(zpool, c + 2)
+                grouped = gpool.tile([P, HG * 4 * SLOTS], BF16, name="grouped", align_bytes=64)
+                nc.scalar.activation(
+                    out=grouped[:].rearrange("p (a u t) -> p a u t", a=HG, t=4),
+                    in_=z_tiles[c][:].rearrange("p a t u -> p a u t"),
+                    func=ACT.Silu,
+                )
+                nc.vector.quantize_mx(
+                    out=h_codes[:, HG * c : HG * (c + 1), :].rearrange("p a u -> p (a u)").bitcast(FP8X4),
+                    scales=h_plane[:, HG * c : HG * (c + 1), :].rearrange("p a u -> p (a u)"),
+                    in_=grouped[:],
+                )
+                for a in range(HG):
+                    if HG * c + a < WHOLE:
+                        passes(HG * c + a, 0, TILES)
         pieces = [(g, 0, CUT[g]) for g in range(WHOLE, GROUPS)] + [(g, CUT[g], TILES) for g in range(WHOLE, GROUPS)]
-        for g, lo, hi in pieces:
-            at = lo
-            for first, count in UNITS:
-                if lo <= first < hi and last_pass[first] == g:
-                    passes(g, at, first + count - at)
-                    at = first + count
-                    leave(first, count)
-            if at < hi:
-                passes(g, at, hi - at)
+        with tc.tile_pool(name="fpool", bufs=1) as fpool:
+            for g, lo, hi in pieces:
+                at = lo
+                for first, count in UNITS:
+                    if lo <= first < hi and last_pass[first] == g:
+                        passes(g, at, first + count - at)
+                        at = first + count
+                        leave(fpool, first, count)
+                if at < hi:
+                    passes(g, at, hi - at)

import concourse.mybir as mybir
from concourse.masks import make_identity

F32 = mybir.dt.float32
BF16 = mybir.dt.bfloat16
I32 = mybir.dt.int32
U32 = mybir.dt.uint32
U8 = mybir.dt.uint8
FP8X4 = mybir.dt.float8_e4m3fn_x4
ALU = mybir.AluOpType
ACT = mybir.ActivationFunctionType
AX = mybir.AxisListType

P = 128
NPTS = 16
HID = 8192
HEADS = 2048
GROUPS = HID // 512
FULL = 1088
SLOTS = 128
TILES = HEADS // P
BANK_TILES = 2
UNITS = ((0, 4), (4, 4), (8, 4), (12, 2), (14, 2))
HG = 2
EARLY = 0
CUT = {9: 4, 10: 8, 11: 8, 12: 12, 13: 12, 14: 14, 15: 14}
WHOLE = GROUPS - len(CUT)
SW_PLANES = (0, 1, 2, 3)
TINY = 1e-30

FLOPS = 2 * NPTS * NPTS * HID * HEADS


def block_views(full, compact, size):
    off = 16 - 2 * size
    nb = 8 // size
    comp = compact.rearrange("p (m b r q) -> p m b r q", b=nb, r=size, q=16)[:, :, :, :, off : off + size]
    by_block = full.rearrange("p (m s x) -> p m s x", s=4 * nb, x=34 * size)[:, :, 0:nb, :]
    upper = by_block[:, :, :, 0 : 16 * size].rearrange("p m b (r y) -> p m b r y", y=16)[:, :, :, :, size : 2 * size]
    lower = by_block[:, :, :, 16 * size : 32 * size].rearrange("p m b (c y) -> p m b c y", y=16)[:, :, :, :, 0:size]
    return comp, upper, lower


def tile_distancerelativebias_w_kernel(tc, coords, w1, b1, w2_words, w2_scales, b2, out):
    nc = tc.nc
    with tc.manual_schedule(), tc.tile_pool(name="keep", bufs=1) as keep, tc.psum_pool(name="psum", bufs=1) as psum:
        cb = keep.tile([P, NPTS * 3], BF16, name="cb")
        nc.scalar.dma_start(out=cb[:], in_=coords.rearrange("b n d -> (b n d)").partition_broadcast(P))
        rows = keep.tile([P, 512], BF16, name="rows")
        nc.scalar.dma_start(out=rows[0:16, :], in_=w1.rearrange("o (g k) -> (o g) k", k=512))
        nc.scalar.dma_start(out=rows[16:32, :], in_=b1.rearrange("(g k) -> g k", k=512))
        b2rows = keep.tile([16, P], BF16, name="b2rows")
        nc.scalar.dma_start(out=b2rows[:], in_=b2.rearrange("(t p) -> t p", p=P))

        planes = keep.tile([P, 4, HEADS], U8, name="planes", align_bytes=256)
        one = keep.tile([P, 1], F32, name="one")
        warm = keep.tile([P, 1], F32, name="warm")
        nc.vector.memset(one[:], 1.0)
        nc.scalar.activation(out=warm[:], in_=one[:], func=ACT.Sqrt)
        for gq in SW_PLANES:
            nc.vector.memset(planes[:, gq, :].bitcast(I32), 0)
        for gq in range(4):
            if gq not in SW_PLANES:
                nc.vector.memset(planes[:, gq, :].bitcast(I32), 0)

        ident = keep.tile([P, P], F32, name="ident")
        make_identity(nc, ident[:])
        nc.vector.memset(rows[32:64, :], 0.0)
        nc.vector.memset(rows[64:128, :], 0.0)
        b2pad = keep.tile([P, P], F32, name="b2pad")
        nc.vector.memset(b2pad[:], 0.0)

        words = {}

        def load_words(g0, g1, first, count):
            wt = keep.tile([P, g1 - g0, P * count], U32, name="w%d_%d" % (g0, first), align_bytes=256)
            src = w2_words[g0:g1].rearrange("g p n t -> p g (n t)")
            nc.sync.dma_start(
                out=wt[:].bitcast(I32), in_=src[:, :, 4 * P * first : 4 * P * (first + count)].bitcast(I32)
            )
            for g in range(g0, g1):
                for tl in range(count):
                    words[(g, first + tl)] = wt[:, g - g0, P * tl : P * (tl + 1)]

        def load_planes(gq):
            for quad in range(4):
                dst = planes[32 * quad : 32 * quad + 16, gq, :]
                src = w2_scales[4 * gq : 4 * gq + 4, 4 * quad : 4 * quad + 4, :]
                if gq in SW_PLANES:
                    nc.gpsimd.dma_start(out=dst.bitcast(F32), in_=src.bitcast(F32))
                else:
                    nc.sync.dma_start(out=dst.bitcast(I32), in_=src.bitcast(I32))

        for g in range(EARLY):
            load_words(g, g + 1, 0, TILES)
        for gq in range(4):
            load_planes(gq)
        for g in range(EARLY, WHOLE):
            load_words(g, g + 1, 0, TILES)
        for g in range(WHOLE, GROUPS):
            load_words(g, g + 1, 0, CUT[g])
        for g in range(WHOLE, GROUPS):
            load_words(g, g + 1, CUT[g], TILES - CUT[g])

        nc.vector.tensor_copy(out=b2pad[0:16, :], in_=b2rows[:])
        pro = psum.tile([P, 512], F32, tag="bank0", name="pro")
        row_words = rows[:].bitcast(F32)
        for u in range(2):
            nc.tensor.transpose(pro[:, P * u : P * (u + 1)], row_words[:, u : 256 : 2], ident[:])
        nc.tensor.transpose(pro[:, 2 * P : 3 * P], b2pad[:], ident[:])

        with tc.tile_pool(name="dpool", bufs=1) as dpool:
            c3 = cb[:].rearrange("p (n c) -> p n c", c=3)
            diff = dpool.tile([P, NPTS, NPTS, 3], F32, name="diff")
            nc.vector.tensor_tensor(
                out=diff[:],
                in0=c3.unsqueeze(2).to_broadcast([P, NPTS, NPTS, 3]),
                in1=c3.unsqueeze(1).to_broadcast([P, NPTS, NPTS, 3]),
                op=ALU.subtract,
            )
            nc.vector.tensor_tensor(out=diff[:], in0=diff[:], in1=diff[:], op=ALU.mult)
            sq_full = dpool.tile([P, FULL], F32, name="sq_full")
            nc.vector.tensor_reduce(
                out=sq_full[:, 0:256], in_=diff[:].rearrange("p i j c -> p (i j) c"), axis=AX.X, op=ALU.add
            )

            wb_bf = keep.tile([P, 32, 4], BF16, name="wb_bf")
            nc.vector.tensor_copy(
                out=wb_bf[:].rearrange("p r t -> p (r t)").bitcast(F32).rearrange("p (r u) -> p r u", u=2),
                in_=pro[:, 0 : 2 * P].rearrange("p (u r) -> p r u", u=2)[:, 0:32, :],
            )
            wb = keep.tile([P, 128], F32, name="wb")
            nc.vector.tensor_copy(out=wb[:], in_=wb_bf[:].rearrange("p r t -> p (r t)"))
            b2col = keep.tile([P, TILES], F32, name="b2col")
            nc.vector.tensor_copy(out=b2col[:], in_=pro[:, 2 * P : 2 * P + TILES])

            sq = keep.tile([P, SLOTS], F32, name="sq")
            for size in (8, 4, 2, 1):
                comp, upper, lower = block_views(sq_full[:], sq[:], size)
                nc.vector.tensor_copy(out=comp, in_=upper)
            nc.vector.tensor_copy(
                out=sq[:].rearrange("p (b q) -> p b q", q=16)[:, :, 15:16],
                in_=sq_full[:].rearrange("p (b x) -> p b x", x=34)[:, 0:8, 0:1],
            )
        safe = keep.tile([P, SLOTS], F32, name="safe")
        nc.vector.tensor_scalar(out=safe[:], in0=sq[:], scalar1=TINY, scalar2=None, op0=ALU.max)
        root = keep.tile([P, SLOTS], F32, name="root")
        nc.scalar.activation(out=root[:], in_=safe[:], func=ACT.Sqrt)
        dist = keep.tile([P, SLOTS], F32, name="dist")
        nc.vector.scalar_tensor_tensor(
            out=dist[:], in0=sq[:], scalar=0.0, in1=root[:], op0=ALU.is_gt, op1=ALU.mult
        )

        h_codes = keep.tile([P, GROUPS, SLOTS], U32, name="h_codes", align_bytes=64)
        h_plane = keep.tile([P, GROUPS, SLOTS], U8, name="h_plane", align_bytes=64)
        z_tiles = {}

        def affine(zpool, c):
            z = zpool.tile([P, HG, 4, SLOTS], F32, name="z")
            for a in range(HG):
                for t in range(4):
                    col = 4 * (HG * c + a) + t
                    nc.vector.tensor_scalar(
                        out=z[:, a, t, :],
                        in0=dist[:],
                        scalar1=wb[:, col : col + 1],
                        scalar2=wb[:, 64 + col : 64 + col + 1],
                        op0=ALU.mult,
                        op1=ALU.add,
                    )
            z_tiles[c] = z

        acc = {}
        last_pass = {}
        for tile_no in range(TILES):
            late = [g for g in range(WHOLE, GROUPS) if tile_no >= CUT[g]]
            last_pass[tile_no] = late[-1] if late else GROUPS - 1

        def passes(g, first, count):
            for tile_no in range(first, first + count):
                place = tile_no % BANK_TILES
                if g == 0 and place == 0:
                    bank = psum.tile([P, 512], F32, tag="bank%d" % (tile_no // BANK_TILES), name="acc%d" % tile_no)
                    for k in range(BANK_TILES):
                        acc[tile_no + k] = bank[:, SLOTS * k : SLOTS * (k + 1)]
                nc.tensor.matmul_mx(
                    out=acc[tile_no],
                    lhsT=words[(g, tile_no)].bitcast(FP8X4),
                    lhsT_scale=planes[4 * (g % 4) : P, g // 4, P * tile_no : P * (tile_no + 1)],
                    rhs=h_codes[:, g, :].bitcast(FP8X4),
                    rhs_scale=h_plane[:, g, :],
                    start=(g == 0 and place == 0),
                    stop=(g == last_pass[tile_no] and place == BANK_TILES - 1),
                )

        out_rows = out.rearrange("b (t p) i j -> p (b t) (i j)", p=P)

        def leave(fpool, first, count):
            compact = keep.tile([P, count * SLOTS], F32, name="compact%d" % first)
            full = fpool.tile([P, count * FULL], F32, name="full%d" % first, align_bytes=256)
            for a in range(count):
                tile_no = first + a
                bias = b2col[:, tile_no : tile_no + 1]
                dst = compact[:, SLOTS * a : SLOTS * (a + 1)]
                if (tile_no // BANK_TILES) % 2 == 0:
                    nc.scalar.activation(out=dst, in_=acc[tile_no], func=ACT.Identity, bias=bias)
                else:
                    nc.vector.tensor_scalar(out=dst, in0=acc[tile_no], scalar1=bias, scalar2=None, op0=ALU.add)
            comp, upper, lower = block_views(full[:], compact[:], 8)
            nc.scalar.copy(out=upper, in_=comp)
            nc.scalar.copy(out=lower, in_=comp.rearrange("p m b r c -> p m b c r"))
            for size in (4, 2):
                comp, upper, lower = block_views(full[:], compact[:], size)
                nc.vector.tensor_copy(out=upper, in_=comp)
                nc.vector.tensor_copy(out=lower, in_=comp.rearrange("p m b r c -> p m b c r"))
            by_two = full[:].rearrange("p (m s x) -> p m s x", s=32, x=34)[:, :, 0:8, :]
            slots = compact[:].rearrange("p (m b q) -> p m b q", b=8, q=16)
            nc.vector.tensor_copy(
                out=by_two[:, :, :, 1:31].rearrange("p m b (a y) -> p m b a y", y=15)[:, :, :, :, 0:1],
                in_=slots[:, :, :, 14:15].unsqueeze(3).to_broadcast([P, count, 8, 2, 1]),
            )
            nc.vector.tensor_copy(
                out=by_two[:, :, :, 0:34].rearrange("p m b (a y) -> p m b a y", y=17)[:, :, :, :, 0:1],
                in_=slots[:, :, :, 15:16].unsqueeze(3).to_broadcast([P, count, 8, 2, 1]),
            )
            nc.sync.dma_start(
                out=out_rows[:, first : first + count, :],
                in_=full[:].rearrange("p (t x) -> p t x", x=FULL)[:, :, 0:256],
            )

        chunks = GROUPS // HG
        with tc.tile_pool(name="zpool", bufs=3) as zpool, tc.tile_pool(name="gpool", bufs=3) as gpool:
            affine(zpool, 0)
            affine(zpool, 1)
            for c in range(chunks):
                if c + 2 < chunks:
                    affine(zpool, c + 2)
                grouped = gpool.tile([P, HG * 4 * SLOTS], BF16, name="grouped", align_bytes=64)
                nc.scalar.activation(
                    out=grouped[:].rearrange("p (a u t) -> p a u t", a=HG, t=4),
                    in_=z_tiles[c][:].rearrange("p a t u -> p a u t"),
                    func=ACT.Silu,
                )
                nc.vector.quantize_mx(
                    out=h_codes[:, HG * c : HG * (c + 1), :].rearrange("p a u -> p (a u)").bitcast(FP8X4),
                    scales=h_plane[:, HG * c : HG * (c + 1), :].rearrange("p a u -> p (a u)"),
                    in_=grouped[:],
                )
                for a in range(HG):
                    if HG * c + a < WHOLE:
                        passes(HG * c + a, 0, TILES)
        pieces = [(g, 0, CUT[g]) for g in range(WHOLE, GROUPS)] + [(g, CUT[g], TILES) for g in range(WHOLE, GROUPS)]
        with tc.tile_pool(name="fpool", bufs=1) as fpool:
            for g, lo, hi in pieces:
                at = lo
                for first, count in UNITS:
                    if lo <= first < hi and last_pass[first] == g:
                        passes(g, at, first + count - at)
                        at = first + count
                        leave(fpool, first, count)
                if at < hi:
                    passes(g, at, hi - at)
